import numpy as np
import ml_dtypes


def mxq(x, axis, fmt="e4m3"):
    dtype, down = {"e4m3": (ml_dtypes.float8_e4m3fn, 7), "e5m2": (ml_dtypes.float8_e5m2, 14)}[fmt]
    v = np.moveaxis(np.asarray(x, np.float32).astype(ml_dtypes.bfloat16).astype(np.float64), axis, -1)
    blocks = v.reshape(v.shape[:-1] + (-1, 32))
    amax = np.abs(blocks).max(-1, keepdims=True)
    byte = np.maximum(np.where(amax > 0, np.frexp(amax)[1] - 1 + 127, 0) - down, 1)
    scale = np.exp2(byte - 127.0)
    codes = (blocks / scale).astype(np.float32).astype(dtype).astype(np.float64)
    return np.moveaxis((codes * scale).reshape(v.shape), -1, axis)


WIDE = False


def mx_kscale(k):
    if not WIDE:
        return np.ones(k)
    levels = np.array([10, -10, 5, -5, 0])
    a = np.random.permutation(np.resize(levels, k // 512 * 4)).reshape(k // 512, 4)
    idx = np.arange(k)
    return np.exp2(a[idx // 512, idx % 128 // 32])


BF16 = ml_dtypes.bfloat16


def bf(x):
    return np.asarray(x, np.float32).astype(BF16)


def f64(x):
    return np.asarray(x).astype(np.float64)


B, S, DIM, H, NKV, HD, GS = 1, 256, 8192, 16, 4, 64, 128
QS = H * HD
KVS = NKV * HD
HALF = HD // 2
ROPE_BASE = 10000.0
RMS_EPS = 1.1920929e-07


def rms_norm(v):
    return v / np.sqrt(np.mean(v * v, axis=-1, keepdims=True) + RMS_EPS)


def rope_cos_sin():
    inv_freq = 1.0 / ROPE_BASE ** (np.arange(0, HD, 2) / HD)
    freqs = np.outer(np.arange(S), inv_freq)
    return np.cos(freqs)[None, :, None, :], np.sin(freqs)[None, :, None, :]


def apply_rotary_emb(u, cos, sin):
    u1, u2 = u[..., :HALF], u[..., HALF:]
    return np.concatenate((u1 * cos + u2 * sin, u1 * -sin + u2 * cos), axis=-1)


def setup_inputs():
    s = mx_kscale(DIM)
    return {"x": bf(np.random.standard_normal((B, S, DIM)) * s),
            "w_qkv_tern": bf(np.random.standard_normal((QS + 2 * KVS, DIM)) * 0.66 / np.sqrt(DIM) / s[None, :]),
            "q_gain": bf(1.0 + 0.1 * np.random.standard_normal(H))}


def reference(x, w_qkv_tern, q_gain):
    qkv = mxq(f64(x), 2, "e4m3") @ mxq(f64(w_qkv_tern), 1, "e4m3").T
    q = qkv[..., :QS].reshape(B, S, H, HD)
    k = qkv[..., QS:QS + KVS].reshape(B, S, NKV, HD)
    v = qkv[..., QS + KVS:].reshape(B, S, NKV, HD)
    q, k = rms_norm(q), rms_norm(k)
    cos, sin = rope_cos_sin()
    q = apply_rotary_emb(q, cos, sin)
    k = apply_rotary_emb(k, cos, sin)
    q = q * f64(q_gain)[None, None, :, None]
    return q, k, v

@@ -1,0 +1,296 @@
+import math
+from contextlib import ExitStack
+
+import concourse.masks as masks
+import concourse.mybir as mybir
+
+F32 = mybir.dt.float32
+BF16 = mybir.dt.bfloat16
+I32 = mybir.dt.int32
+U32 = mybir.dt.uint32
+U8 = mybir.dt.uint8
+FP8X4 = mybir.dt.float8_e4m3fn_x4
+ALU = mybir.AluOpType
+ACT = mybir.ActivationFunctionType
+AXIS = mybir.AxisListType
+
+P = 128
+PACK = 4
+K_PASS = P * PACK
+PLANES = 2
+
+TOKENS = 256
+DIM = 8192
+HEAD = 64
+HALF = HEAD // 2
+Q_HEADS = 16
+ROPE_BASE = 10000.0
+RMS_EPS = 1.1920929e-07
+
+ROW_TILES = 2
+GROUP_ROWS = ROW_TILES * P
+TOKEN_TILES = TOKENS // P
+CHUNK_PASSES = 4
+CHUNK_K = CHUNK_PASSES * K_PASS
+K_PARTS = DIM // CHUNK_K
+HEADS_PER_ROUND = GROUP_ROWS // HEAD
+ROUND_HEADS = TOKEN_TILES * HEADS_PER_ROUND
+Q_ROUNDS = Q_HEADS // HEADS_PER_ROUND
+K_ROUND = Q_ROUNDS
+V_ROUND = Q_ROUNDS + 1
+ROUNDS = Q_ROUNDS + 2
+
+PREFETCH = 8
+RAW_BUFS = PREFETCH + 1
+MULTIPLY_LAG = 2
+QUANT_PASSES = 2
+QUANTS = CHUNK_PASSES // QUANT_PASSES
+TRANSPOSE_BANKS = 6
+VECTOR_EVERY = 8
+
+FLOPS = 2 * TOKENS * DIM * (Q_HEADS + 8) * HEAD
+
+TWO_PI = 2.0 * math.pi
+TWO_PI_HIGH = 6.283203125
+TWO_PI_MID = -1.7814338207244873e-05
+TWO_PI_LOW = TWO_PI - TWO_PI_HIGH - TWO_PI_MID
+ROUND_MAGIC = 12582912.0
+SIN_LIMIT = 3.1415925
+
+
+def tile_causalselfattention_pa_k_kernel(tc, x, w_qkv_tern, q_gain, out_0, out_1, out_2):
+    nc = tc.nc
+
+    x_rows = x.rearrange("b (j p) k -> p (b j) k", p=P)
+    w_rows = w_qkv_tern.rearrange("(r j p) k -> r p j k", j=ROW_TILES, p=P)
+    q_out = out_0.rearrange("b (m p) h d -> p (b m) (h d)", p=P)
+    k_out = out_1.rearrange("b (m p) h d -> p (b m) (h d)", p=P)
+    v_out = out_2.rearrange("b (m p) h d -> p (b m) (h d)", p=P)
+
+    chunks = []
+    for part in range(K_PARTS):
+        chunks.append((None, part))
+        chunks.append((0, part))
+    for rnd in range(1, ROUNDS):
+        for part in range(K_PARTS):
+            chunks.append((rnd, part))
+
+    with ExitStack() as ctx:
+        const = ctx.enter_context(tc.tile_pool(name="const", bufs=1))
+        raw_pool = ctx.enter_context(tc.tile_pool(name="raw", bufs=RAW_BUFS))
+        grouped_pool = ctx.enter_context(tc.tile_pool(name="grouped", bufs=6))
+        w_pool = ctx.enter_context(tc.tile_pool(name="w_mx", bufs=MULTIPLY_LAG + 2))
+        post = ctx.enter_context(tc.tile_pool(name="post", bufs=2))
+        bank_pool = ctx.enter_context(tc.psum_pool(name="banks", bufs=TRANSPOSE_BANKS))
+        sum_pool = ctx.enter_context(tc.psum_pool(name="sums", bufs=1))
+        ctx.enter_context(tc.manual_schedule())
+
+        raws = {}
+        mx = {}
+        x_mx = {}
+        sums = {}
+        held = {}
+
+        def load(i):
+            rnd, part = chunks[i]
+            rows = x_rows if rnd is None else w_rows[rnd]
+            raw = raw_pool.tile([P, ROW_TILES * CHUNK_K], BF16)
+            raw_rows = raw[:].rearrange("p (j k) -> p j k", j=ROW_TILES)
+            nc.sync.dma_start(out=raw_rows, in_=rows[:, :, part * CHUNK_K : (part + 1) * CHUNK_K])
+            raws[i] = raw
+
+        def quantise(grouped, words, scales, n):
+            cols = slice(n * QUANT_PASSES * GROUP_ROWS, (n + 1) * QUANT_PASSES * GROUP_ROWS)
+            nc.vector.quantize_mx(
+                out=words[:, cols].bitcast(FP8X4), scales=scales[:, cols], in_=grouped[:]
+            )
+
+        def stage(i):
+            rnd, part = chunks[i]
+            pool = const if rnd is None else w_pool
+            words = pool.tile(
+                [P, CHUNK_PASSES * GROUP_ROWS], U32, align_bytes=64,
+                name="x_words%d" % part if rnd is None else "w_words",
+            )
+            scales = pool.tile(
+                [P, CHUNK_PASSES * GROUP_ROWS], U8, align_bytes=64,
+                name="x_scales%d" % part if rnd is None else "w_scales",
+            )
+            if rnd is None:
+                x_mx[part] = (words, scales)
+            else:
+                mx[i] = (words, scales)
+            raw_words = raws[i][:].bitcast(F32).rearrange("p (j w) -> p j w", j=ROW_TILES)
+            waiting = None
+            for n in range(QUANTS):
+                grouped = grouped_pool.tile([P, QUANT_PASSES * GROUP_ROWS * PACK], BF16, align_bytes=64)
+                grouped_words = grouped[:].bitcast(F32).rearrange(
+                    "p (c j n u) -> p c j n u", c=QUANT_PASSES, j=ROW_TILES, u=PLANES
+                )
+                for c in range(QUANT_PASSES):
+                    g = n * QUANT_PASSES + c
+                    bank = bank_pool.tile([P, ROW_TILES, PLANES, P], F32)
+                    for j in range(ROW_TILES):
+                        for u in range(PLANES):
+                            w0 = (g * PLANES + u) * P
+                            nc.tensor.transpose(
+                                out=bank[:, j, u, :], in_=raw_words[:, j, w0 : w0 + P], identity=ident[:]
+                            )
+                    to_vector = (part * CHUNK_PASSES + g) % VECTOR_EVERY == VECTOR_EVERY - 1
+                    empty = nc.vector.tensor_copy if to_vector else nc.scalar.copy
+                    empty(out=grouped_words[:, c], in_=bank[:].rearrange("p j u n -> p j n u"))
+                if waiting is not None:
+                    quantise(waiting, words, scales, n - 1)
+                waiting = grouped
+            quantise(waiting, words, scales, QUANTS - 1)
+
+        def multiply(i):
+            rnd, part = chunks[i]
+            if part == 0:
+                sums[rnd] = [
+                    sum_pool.tile([P, GROUP_ROWS], F32, name="sum%d" % m) for m in range(TOKEN_TILES)
+                ]
+            w_words, w_scales = mx[i]
+            x_words, x_scales = x_mx[part]
+            for g in range(CHUNK_PASSES):
+                w_cols = slice(g * GROUP_ROWS, (g + 1) * GROUP_ROWS)
+                for m in range(TOKEN_TILES):
+                    x_cols = slice(g * TOKENS + m * P, g * TOKENS + (m + 1) * P)
+                    nc.tensor.matmul_mx(
+                        out=sums[rnd][m][:],
+                        lhsT=x_words[:, x_cols].bitcast(FP8X4),
+                        lhsT_scale=x_scales[:, x_cols],
+                        rhs=w_words[:, w_cols].bitcast(FP8X4),
+                        rhs_scale=w_scales[:, w_cols],
+                        start=(part == 0 and g == 0),
+                        stop=(part == K_PARTS - 1 and g == CHUNK_PASSES - 1),
+                    )
+
+        def leave_psum(rnd):
+            acc = sums[rnd]
+            if rnd == V_ROUND:
+                result = post.tile([P, TOKEN_TILES, GROUP_ROWS], F32, name="result")
+                nc.scalar.copy(out=result[:, 0, :], in_=acc[0][:])
+                nc.vector.tensor_copy(out=result[:, 1, :], in_=acc[1][:])
+                nc.sync.dma_start(out=v_out, in_=result[:])
+                return
+            squares = post.tile([P, ROUND_HEADS, HEAD], F32)
+            with_cos = post.tile([P, ROUND_HEADS, 2, HALF], F32)
+            with_sin = post.tile([P, ROUND_HEADS, 2, HALF], F32)
+            sum_sq = post.tile([P, ROUND_HEADS], F32)
+            for m in range(TOKEN_TILES):
+                heads = slice(m * HEADS_PER_ROUND, (m + 1) * HEADS_PER_ROUND)
+                u = acc[m][:].rearrange("p (h d) -> p h d", d=HEAD)
+                shape = [P, HEADS_PER_ROUND, HEAD]
+                nc.scalar.activation(out=squares[:, heads, :], in_=u, func=ACT.Square)
+                nc.vector.tensor_tensor(
+                    out=with_cos[:, heads].rearrange("p h s j -> p h (s j)"),
+                    in0=u, in1=cos_cos[:, m : m + 1, :].to_broadcast(shape), op=ALU.mult,
+                )
+                nc.vector.tensor_tensor(
+                    out=with_sin[:, heads].rearrange("p h s j -> p h (s j)"),
+                    in0=u, in1=minus_plus_sin[:, m : m + 1, :].to_broadcast(shape), op=ALU.mult,
+                )
+            nc.vector.tensor_reduce(out=sum_sq[:], in_=squares[:], axis=AXIS.X, op=ALU.add)
+            held[rnd] = (with_cos, with_sin, sum_sq)
+
+        def finish(rnd):
+            with_cos, with_sin, sum_sq = held[rnd]
+            norm = post.tile([P, ROUND_HEADS], F32)
+            factor = post.tile([P, ROUND_HEADS], F32)
+            rotated = post.tile([P, ROUND_HEADS, 2, HALF], F32)
+            result = post.tile([P, TOKEN_TILES, GROUP_ROWS], F32, name="result")
+            nc.scalar.activation(
+                out=norm[:], in_=sum_sq[:], func=ACT.Sqrt, scale=1.0 / HEAD, bias=eps[:, 0:1]
+            )
+            nc.vector.reciprocal(out=factor[:], in_=norm[:])
+            nc.vector.tensor_tensor(
+                out=rotated[:, :, 0, :], in0=with_cos[:, :, 0, :], in1=with_sin[:, :, 1, :], op=ALU.add
+            )
+            if rnd < Q_ROUNDS:
+                by_tile = factor[:].rearrange("p (m h) -> p m h", m=TOKEN_TILES)
+                h0 = rnd * HEADS_PER_ROUND
+                nc.vector.tensor_tensor(
+                    out=by_tile, in0=by_tile,
+                    in1=gain[:, h0 : h0 + HEADS_PER_ROUND].unsqueeze(1).to_broadcast(
+                        [P, TOKEN_TILES, HEADS_PER_ROUND]
+                    ),
+                    op=ALU.mult,
+                )
+            nc.vector.tensor_tensor(
+                out=rotated[:, :, 1, :], in0=with_cos[:, :, 1, :], in1=with_sin[:, :, 0, :], op=ALU.add
+            )
+            nc.vector.tensor_tensor(
+                out=result[:].rearrange("p m (h d) -> p (m h) d", d=HEAD),
+                in0=rotated[:].rearrange("p g s j -> p g (s j)"),
+                in1=factor[:].unsqueeze(2).to_broadcast([P, ROUND_HEADS, HEAD]),
+                op=ALU.mult,
+            )
+            if rnd < Q_ROUNDS:
+                out_cols = q_out[:, :, rnd * GROUP_ROWS : (rnd + 1) * GROUP_ROWS]
+            else:
+                out_cols = k_out
+            nc.gpsimd.dma_start(out=out_cols, in_=result[:])
+
+        for i in range(PREFETCH):
+            load(i)
+
+        ident = const.tile([P, P], F32)
+        masks.make_identity(nc, ident[:])
+        gain_bf = const.tile([P, Q_HEADS], BF16)
+        nc.scalar.dma_start(out=gain_bf[:], in_=q_gain.partition_broadcast(P))
+        eps = const.tile([P, 1], F32)
+        nc.vector.memset(eps[:], RMS_EPS)
+
+        position_i = const.tile([P, TOKEN_TILES], I32)
+        nc.gpsimd.iota(position_i[:], pattern=[[P, TOKEN_TILES]], base=0, channel_multiplier=1)
+        position = const.tile([P, TOKEN_TILES], F32)
+        nc.vector.tensor_copy(out=position[:], in_=position_i[:])
+        angle = const.tile([P, TOKEN_TILES, HALF], F32)
+        for j in range(HALF):
+            nc.vector.tensor_scalar_mul(
+                out=angle[:, :, j], in0=position[:], scalar1=ROPE_BASE ** (-2.0 * j / HEAD)
+            )
+        turns = const.tile([P, TOKEN_TILES, HALF], F32)
+        nc.vector.tensor_scalar(
+            out=turns[:], in0=angle[:], scalar1=1.0 / TWO_PI, scalar2=ROUND_MAGIC, op0=ALU.mult, op1=ALU.add
+        )
+        nc.vector.tensor_scalar_sub(out=turns[:], in0=turns[:], scalar1=ROUND_MAGIC)
+        for piece in (TWO_PI_HIGH, TWO_PI_MID, TWO_PI_LOW):
+            nc.vector.scalar_tensor_tensor(
+                out=angle[:], in0=turns[:], scalar=-piece, in1=angle[:], op0=ALU.mult, op1=ALU.add
+            )
+        nc.vector.tensor_scalar(
+            out=angle[:], in0=angle[:], scalar1=SIN_LIMIT, scalar2=-SIN_LIMIT, op0=ALU.min, op1=ALU.max
+        )
+        minus_plus_sin = const.tile([P, TOKEN_TILES, HEAD], F32)
+        cos_cos = const.tile([P, TOKEN_TILES, HEAD], F32)
+        sin_half = const.tile([P, TOKEN_TILES, HALF], F32)
+        nc.scalar.activation(out=sin_half[:], in_=angle[:], func=ACT.Sin, scale=0.5)
+        nc.scalar.activation(out=minus_plus_sin[:, :, :HALF], in_=angle[:], func=ACT.Sin, scale=-1.0)
+        nc.scalar.activation(out=minus_plus_sin[:, :, HALF:], in_=angle[:], func=ACT.Sin)
+        nc.vector.tensor_tensor(out=sin_half[:], in0=sin_half[:], in1=sin_half[:], op=ALU.mult)
+        for s in range(2):
+            nc.vector.tensor_scalar(
+                out=cos_cos[:, :, s * HALF : (s + 1) * HALF], in0=sin_half[:],
+                scalar1=-2.0, scalar2=1.0, op0=ALU.mult, op1=ALU.add,
+            )
+
+        gain = const.tile([P, Q_HEADS], F32)
+        nc.vector.tensor_copy(out=gain[:], in_=gain_bf[:])
+
+        def closes(i):
+            return 0 <= i < len(chunks) and chunks[i][0] is not None and chunks[i][1] == K_PARTS - 1
+
+        for i in range(len(chunks) + MULTIPLY_LAG):
+            if i + PREFETCH < len(chunks):
+                load(i + PREFETCH)
+            if i < len(chunks):
+                stage(i)
+            ready = i - MULTIPLY_LAG
+            if ready >= 0 and chunks[ready][0] is not None:
+                multiply(ready)
+            if closes(ready):
+                leave_psum(chunks[ready][0])
+            if closes(ready - 1) and chunks[ready - 1][0] != V_ROUND:
+                finish(chunks[ready - 1][0])

@@ -42,7 +42,8 @@ ROUNDS = Q_ROUNDS + 2
 
 PREFETCH = 8
 RAW_BUFS = PREFETCH + 1
-MULTIPLY_LAG = 2
+RUN_PARTS = 2
+W_BUFS = 5
 QUANT_PASSES = 2
 QUANTS = CHUNK_PASSES // QUANT_PASSES
 TRANSPOSE_BANKS = 6
@@ -79,7 +80,7 @@ def tile_causalselfattention_pa_k_kernel(tc, x, w_qkv_tern, q_gain, out_0, out_1
         const = ctx.enter_context(tc.tile_pool(name="const", bufs=1))
         raw_pool = ctx.enter_context(tc.tile_pool(name="raw", bufs=RAW_BUFS))
         grouped_pool = ctx.enter_context(tc.tile_pool(name="grouped", bufs=6))
-        w_pool = ctx.enter_context(tc.tile_pool(name="w_mx", bufs=MULTIPLY_LAG + 2))
+        w_pool = ctx.enter_context(tc.tile_pool(name="w_mx", bufs=W_BUFS))
         post = ctx.enter_context(tc.tile_pool(name="post", bufs=2))
         bank_pool = ctx.enter_context(tc.psum_pool(name="banks", bufs=TRANSPOSE_BANKS))
         sum_pool = ctx.enter_context(tc.psum_pool(name="sums", bufs=1))
@@ -279,18 +280,24 @@ def tile_causalselfattention_pa_k_kernel(tc, x, w_qkv_tern, q_gain, out_0, out_1
         gain = const.tile([P, Q_HEADS], F32)
         nc.vector.tensor_copy(out=gain[:], in_=gain_bf[:])
 
-        def closes(i):
-            return 0 <= i < len(chunks) and chunks[i][0] is not None and chunks[i][1] == K_PARTS - 1
-
-        for i in range(len(chunks) + MULTIPLY_LAG):
+        to_finish = None
+        for i in range(len(chunks) + 1):
             if i + PREFETCH < len(chunks):
                 load(i + PREFETCH)
             if i < len(chunks):
                 stage(i)
-            ready = i - MULTIPLY_LAG
-            if ready >= 0 and chunks[ready][0] is not None:
-                multiply(ready)
-            if closes(ready):
-                leave_psum(chunks[ready][0])
-            if closes(ready - 1) and chunks[ready - 1][0] != V_ROUND:
-                finish(chunks[ready - 1][0])
+            if to_finish is not None:
+                finish(to_finish)
+                to_finish = None
+            if i == 0 or chunks[i - 1][0] is None:
+                continue
+            rnd, part = chunks[i - 1]
+            if rnd == 0:
+                multiply(i - 1)
+            elif part % RUN_PARTS == RUN_PARTS - 1:
+                for j in range(i - RUN_PARTS, i):
+                    multiply(j)
+            if part == K_PARTS - 1:
+                leave_psum(rnd)
+                if rnd != V_ROUND:
+                    to_finish = rnd

@@ -44,6 +44,7 @@ PREFETCH = 8
 RAW_BUFS = PREFETCH + 1
 RUN_PARTS = 2
 W_BUFS = 5
+MX_ALIGN = 256
 QUANT_PASSES = 2
 QUANTS = CHUNK_PASSES // QUANT_PASSES
 TRANSPOSE_BANKS = 6
@@ -82,6 +83,7 @@ def tile_causalselfattention_pa_k_kernel(tc, x, w_qkv_tern, q_gain, out_0, out_1
         grouped_pool = ctx.enter_context(tc.tile_pool(name="grouped", bufs=6))
         w_pool = ctx.enter_context(tc.tile_pool(name="w_mx", bufs=W_BUFS))
         post = ctx.enter_context(tc.tile_pool(name="post", bufs=2))
+        result_pool = ctx.enter_context(tc.tile_pool(name="results", bufs=ROUNDS))
         bank_pool = ctx.enter_context(tc.psum_pool(name="banks", bufs=TRANSPOSE_BANKS))
         sum_pool = ctx.enter_context(tc.psum_pool(name="sums", bufs=1))
         ctx.enter_context(tc.manual_schedule())
@@ -90,7 +92,6 @@ def tile_causalselfattention_pa_k_kernel(tc, x, w_qkv_tern, q_gain, out_0, out_1
         mx = {}
         x_mx = {}
         sums = {}
-        held = {}
 
         def load(i):
             rnd, part = chunks[i]
@@ -110,11 +111,11 @@ def tile_causalselfattention_pa_k_kernel(tc, x, w_qkv_tern, q_gain, out_0, out_1
             rnd, part = chunks[i]
             pool = const if rnd is None else w_pool
             words = pool.tile(
-                [P, CHUNK_PASSES * GROUP_ROWS], U32, align_bytes=64,
+                [P, CHUNK_PASSES * GROUP_ROWS], U32, align_bytes=MX_ALIGN,
                 name="x_words%d" % part if rnd is None else "w_words",
             )
             scales = pool.tile(
-                [P, CHUNK_PASSES * GROUP_ROWS], U8, align_bytes=64,
+                [P, CHUNK_PASSES * GROUP_ROWS], U8, align_bytes=MX_ALIGN,
                 name="x_scales%d" % part if rnd is None else "w_scales",
             )
             if rnd is None:
@@ -124,7 +125,7 @@ def tile_causalselfattention_pa_k_kernel(tc, x, w_qkv_tern, q_gain, out_0, out_1
             raw_words = raws[i][:].bitcast(F32).rearrange("p (j w) -> p j w", j=ROW_TILES)
             waiting = None
             for n in range(QUANTS):
-                grouped = grouped_pool.tile([P, QUANT_PASSES * GROUP_ROWS * PACK], BF16, align_bytes=64)
+                grouped = grouped_pool.tile([P, QUANT_PASSES * GROUP_ROWS * PACK], BF16, align_bytes=MX_ALIGN)
                 grouped_words = grouped[:].bitcast(F32).rearrange(
                     "p (c j n u) -> p c j n u", c=QUANT_PASSES, j=ROW_TILES, u=PLANES
                 )
@@ -167,19 +168,23 @@ def tile_causalselfattention_pa_k_kernel(tc, x, w_qkv_tern, q_gain, out_0, out_1
                         stop=(part == K_PARTS - 1 and g == CHUNK_PASSES - 1),
                     )
 
-        def leave_psum(rnd):
+        def v_leaves(rnd):
             acc = sums[rnd]
-            if rnd == V_ROUND:
-                result = post.tile([P, TOKEN_TILES, GROUP_ROWS], F32, name="result")
-                nc.scalar.copy(out=result[:, 0, :], in_=acc[0][:])
-                nc.vector.tensor_copy(out=result[:, 1, :], in_=acc[1][:])
-                nc.sync.dma_start(out=v_out, in_=result[:])
-                return
+            result = result_pool.tile([P, TOKEN_TILES, GROUP_ROWS], F32)
+            nc.scalar.copy(out=result[:, 0, :], in_=acc[0][:])
+            nc.vector.tensor_copy(out=result[:, 1, :], in_=acc[1][:])
+            nc.sync.dma_start(out=v_out, in_=result[:])
+
+        def epilogue(rnd):
+            acc = sums[rnd]
             squares = post.tile([P, ROUND_HEADS, HEAD], F32)
             with_cos = post.tile([P, ROUND_HEADS, 2, HALF], F32)
             with_sin = post.tile([P, ROUND_HEADS, 2, HALF], F32)
+            rotated = post.tile([P, ROUND_HEADS, 2, HALF], F32)
             sum_sq = post.tile([P, ROUND_HEADS], F32)
-            for m in range(TOKEN_TILES):
+            factor = post.tile([P, ROUND_HEADS], F32)
+
+            def leave_psum(m):
                 heads = slice(m * HEADS_PER_ROUND, (m + 1) * HEADS_PER_ROUND)
                 u = acc[m][:].rearrange("p (h d) -> p h d", d=HEAD)
                 shape = [P, HEADS_PER_ROUND, HEAD]
@@ -192,46 +197,50 @@ def tile_causalselfattention_pa_k_kernel(tc, x, w_qkv_tern, q_gain, out_0, out_1
                     out=with_sin[:, heads].rearrange("p h s j -> p h (s j)"),
                     in0=u, in1=minus_plus_sin[:, m : m + 1, :].to_broadcast(shape), op=ALU.mult,
                 )
-            nc.vector.tensor_reduce(out=sum_sq[:], in_=squares[:], axis=AXIS.X, op=ALU.add)
-            held[rnd] = (with_cos, with_sin, sum_sq)
 
-        def finish(rnd):
-            with_cos, with_sin, sum_sq = held[rnd]
-            norm = post.tile([P, ROUND_HEADS], F32)
-            factor = post.tile([P, ROUND_HEADS], F32)
-            rotated = post.tile([P, ROUND_HEADS, 2, HALF], F32)
-            result = post.tile([P, TOKEN_TILES, GROUP_ROWS], F32, name="result")
-            nc.scalar.activation(
-                out=norm[:], in_=sum_sq[:], func=ACT.Sqrt, scale=1.0 / HEAD, bias=eps[:, 0:1]
-            )
-            nc.vector.reciprocal(out=factor[:], in_=norm[:])
-            nc.vector.tensor_tensor(
-                out=rotated[:, :, 0, :], in0=with_cos[:, :, 0, :], in1=with_sin[:, :, 1, :], op=ALU.add
-            )
-            if rnd < Q_ROUNDS:
-                by_tile = factor[:].rearrange("p (m h) -> p m h", m=TOKEN_TILES)
-                h0 = rnd * HEADS_PER_ROUND
+            def first_share():
+                for m in range(TOKEN_TILES):
+                    leave_psum(m)
+
+            def second_share():
+                nc.vector.tensor_reduce(out=sum_sq[:], in_=squares[:], axis=AXIS.X, op=ALU.add)
+
                 nc.vector.tensor_tensor(
-                    out=by_tile, in0=by_tile,
-                    in1=gain[:, h0 : h0 + HEADS_PER_ROUND].unsqueeze(1).to_broadcast(
-                        [P, TOKEN_TILES, HEADS_PER_ROUND]
-                    ),
+                    out=rotated[:, :, 0, :], in0=with_cos[:, :, 0, :], in1=with_sin[:, :, 1, :], op=ALU.add
+                )
+                nc.vector.tensor_tensor(
+                    out=rotated[:, :, 1, :], in0=with_cos[:, :, 1, :], in1=with_sin[:, :, 0, :], op=ALU.add
+                )
+
+            def third_share():
+                result = result_pool.tile([P, TOKEN_TILES, GROUP_ROWS], F32)
+                nc.scalar.activation(
+                    out=factor[:], in_=sum_sq[:], func=ACT.Sqrt, scale=1.0 / HEAD, bias=eps[:, 0:1]
+                )
+                nc.vector.reciprocal(out=factor[:], in_=factor[:])
+                if rnd < Q_ROUNDS:
+                    by_tile = factor[:].rearrange("p (m h) -> p m h", m=TOKEN_TILES)
+                    h0 = rnd * HEADS_PER_ROUND
+                    nc.vector.tensor_tensor(
+                        out=by_tile, in0=by_tile,
+                        in1=gain[:, h0 : h0 + HEADS_PER_ROUND].unsqueeze(1).to_broadcast(
+                            [P, TOKEN_TILES, HEADS_PER_ROUND]
+                        ),
+                        op=ALU.mult,
+                    )
+                nc.vector.tensor_tensor(
+                    out=result[:].rearrange("p m (h d) -> p (m h) d", d=HEAD),
+                    in0=rotated[:].rearrange("p g s j -> p g (s j)"),
+                    in1=factor[:].unsqueeze(2).to_broadcast([P, ROUND_HEADS, HEAD]),
                     op=ALU.mult,
                 )
-            nc.vector.tensor_tensor(
-                out=rotated[:, :, 1, :], in0=with_cos[:, :, 1, :], in1=with_sin[:, :, 0, :], op=ALU.add
-            )
-            nc.vector.tensor_tensor(
-                out=result[:].rearrange("p m (h d) -> p (m h) d", d=HEAD),
-                in0=rotated[:].rearrange("p g s j -> p g (s j)"),
-                in1=factor[:].unsqueeze(2).to_broadcast([P, ROUND_HEADS, HEAD]),
-                op=ALU.mult,
-            )
-            if rnd < Q_ROUNDS:
-                out_cols = q_out[:, :, rnd * GROUP_ROWS : (rnd + 1) * GROUP_ROWS]
-            else:
-                out_cols = k_out
-            nc.gpsimd.dma_start(out=out_cols, in_=result[:])
+                if rnd < Q_ROUNDS:
+                    out_cols = q_out[:, :, rnd * GROUP_ROWS : (rnd + 1) * GROUP_ROWS]
+                else:
+                    out_cols = k_out
+                nc.gpsimd.dma_start(out=out_cols, in_=result[:])
+
+            return [first_share, second_share, third_share]
 
         for i in range(PREFETCH):
             load(i)
@@ -280,15 +289,14 @@ def tile_causalselfattention_pa_k_kernel(tc, x, w_qkv_tern, q_gain, out_0, out_1
         gain = const.tile([P, Q_HEADS], F32)
         nc.vector.tensor_copy(out=gain[:], in_=gain_bf[:])
 
-        to_finish = None
+        shares = []
         for i in range(len(chunks) + 1):
             if i + PREFETCH < len(chunks):
                 load(i + PREFETCH)
             if i < len(chunks):
                 stage(i)
-            if to_finish is not None:
-                finish(to_finish)
-                to_finish = None
+            if shares:
+                shares.pop(0)()
             if i == 0 or chunks[i - 1][0] is None:
                 continue
             rnd, part = chunks[i - 1]
@@ -298,6 +306,8 @@ def tile_causalselfattention_pa_k_kernel(tc, x, w_qkv_tern, q_gain, out_0, out_1
                 for j in range(i - RUN_PARTS, i):
                     multiply(j)
             if part == K_PARTS - 1:
-                leave_psum(rnd)
-                if rnd != V_ROUND:
-                    to_finish = rnd
+                if rnd == V_ROUND:
+                    v_leaves(rnd)
+                else:
+                    shares = epilogue(rnd)
+                    shares.pop(0)()

@@ -5,8 +5,8 @@ import concourse.masks as masks
 import concourse.mybir as mybir
 
 F32 = mybir.dt.float32
-BF16 = mybir.dt.bfloat16
 I32 = mybir.dt.int32
+BF16 = mybir.dt.bfloat16
 U32 = mybir.dt.uint32
 U8 = mybir.dt.uint8
 FP8X4 = mybir.dt.float8_e4m3fn_x4
@@ -25,6 +25,7 @@ HEAD = 64
 HALF = HEAD // 2
 Q_HEADS = 16
 ROPE_BASE = 10000.0
+ANGLES_ALONE = 8
 RMS_EPS = 1.1920929e-07
 
 ROW_TILES = 2
@@ -46,7 +47,6 @@ RUN_PARTS = 2
 W_BUFS = 5
 MX_ALIGN = 256
 QUANT_PASSES = 2
-QUANTS = CHUNK_PASSES // QUANT_PASSES
 TRANSPOSE_BANKS = 6
 VECTOR_EVERY = 8
 
@@ -101,8 +101,8 @@ def tile_causalselfattention_pa_k_kernel(tc, x, w_qkv_tern, q_gain, out_0, out_1
             nc.sync.dma_start(out=raw_rows, in_=rows[:, :, part * CHUNK_K : (part + 1) * CHUNK_K])
             raws[i] = raw
 
-        def quantise(grouped, words, scales, n):
-            cols = slice(n * QUANT_PASSES * GROUP_ROWS, (n + 1) * QUANT_PASSES * GROUP_ROWS)
+        def quantise(grouped, words, scales, n, size):
+            cols = slice(n * size * GROUP_ROWS, (n + 1) * size * GROUP_ROWS)
             nc.vector.quantize_mx(
                 out=words[:, cols].bitcast(FP8X4), scales=scales[:, cols], in_=grouped[:]
             )
@@ -124,13 +124,15 @@ def tile_causalselfattention_pa_k_kernel(tc, x, w_qkv_tern, q_gain, out_0, out_1
                 mx[i] = (words, scales)
             raw_words = raws[i][:].bitcast(F32).rearrange("p (j w) -> p j w", j=ROW_TILES)
             waiting = None
-            for n in range(QUANTS):
-                grouped = grouped_pool.tile([P, QUANT_PASSES * GROUP_ROWS * PACK], BF16, align_bytes=MX_ALIGN)
+            is_last = i == len(chunks) - 1
+            size = 1 if is_last else QUANT_PASSES
+            for n in range(CHUNK_PASSES // size):
+                grouped = grouped_pool.tile([P, size * GROUP_ROWS * PACK], BF16, align_bytes=MX_ALIGN)
                 grouped_words = grouped[:].bitcast(F32).rearrange(
-                    "p (c j n u) -> p c j n u", c=QUANT_PASSES, j=ROW_TILES, u=PLANES
+                    "p (c j n u) -> p c j n u", c=size, j=ROW_TILES, u=PLANES
                 )
-                for c in range(QUANT_PASSES):
-                    g = n * QUANT_PASSES + c
+                for c in range(size):
+                    g = n * size + c
                     bank = bank_pool.tile([P, ROW_TILES, PLANES, P], F32)
                     for j in range(ROW_TILES):
                         for u in range(PLANES):
@@ -138,13 +140,13 @@ def tile_causalselfattention_pa_k_kernel(tc, x, w_qkv_tern, q_gain, out_0, out_1
                             nc.tensor.transpose(
                                 out=bank[:, j, u, :], in_=raw_words[:, j, w0 : w0 + P], identity=ident[:]
                             )
-                    to_vector = (part * CHUNK_PASSES + g) % VECTOR_EVERY == VECTOR_EVERY - 1
+                    to_vector = g == 1 if is_last else (part * CHUNK_PASSES + g) % VECTOR_EVERY == VECTOR_EVERY - 1
                     empty = nc.vector.tensor_copy if to_vector else nc.scalar.copy
                     empty(out=grouped_words[:, c], in_=bank[:].rearrange("p j u n -> p j n u"))
                 if waiting is not None:
-                    quantise(waiting, words, scales, n - 1)
+                    quantise(waiting, words, scales, n - 1, size)
                 waiting = grouped
-            quantise(waiting, words, scales, QUANTS - 1)
+            quantise(waiting, words, scales, n, size)
 
         def multiply(i):
             rnd, part = chunks[i]
@@ -170,16 +172,17 @@ def tile_causalselfattention_pa_k_kernel(tc, x, w_qkv_tern, q_gain, out_0, out_1
 
         def v_leaves(rnd):
             acc = sums[rnd]
-            result = result_pool.tile([P, TOKEN_TILES, GROUP_ROWS], F32)
-            nc.scalar.copy(out=result[:, 0, :], in_=acc[0][:])
-            nc.vector.tensor_copy(out=result[:, 1, :], in_=acc[1][:])
-            nc.sync.dma_start(out=v_out, in_=result[:])
+            halves = [post.tile([P, GROUP_ROWS], F32, name="v_result%d" % m) for m in range(TOKEN_TILES)]
+            nc.scalar.copy(out=halves[0][:], in_=acc[0][:])
+            nc.vector.tensor_copy(out=halves[1][:], in_=acc[1][:])
+            nc.scalar.dma_start(out=v_out[:, 0, :], in_=halves[0][:])
+            nc.sync.dma_start(out=v_out[:, 1, :], in_=halves[1][:])
 
         def epilogue(rnd):
             acc = sums[rnd]
             squares = post.tile([P, ROUND_HEADS, HEAD], F32)
-            with_cos = post.tile([P, ROUND_HEADS, 2, HALF], F32)
-            with_sin = post.tile([P, ROUND_HEADS, 2, HALF], F32)
+            products = post.tile([P, 2, ROUND_HEADS, HEAD], F32)
+            by_half = products[:].rearrange("p t h (s j) -> p t h s j", s=2)
             rotated = post.tile([P, ROUND_HEADS, 2, HALF], F32)
             sum_sq = post.tile([P, ROUND_HEADS], F32)
             factor = post.tile([P, ROUND_HEADS], F32)
@@ -187,15 +190,11 @@ def tile_causalselfattention_pa_k_kernel(tc, x, w_qkv_tern, q_gain, out_0, out_1
             def leave_psum(m):
                 heads = slice(m * HEADS_PER_ROUND, (m + 1) * HEADS_PER_ROUND)
                 u = acc[m][:].rearrange("p (h d) -> p h d", d=HEAD)
-                shape = [P, HEADS_PER_ROUND, HEAD]
+                shape = [P, 2, HEADS_PER_ROUND, HEAD]
                 nc.scalar.activation(out=squares[:, heads, :], in_=u, func=ACT.Square)
                 nc.vector.tensor_tensor(
-                    out=with_cos[:, heads].rearrange("p h s j -> p h (s j)"),
-                    in0=u, in1=cos_cos[:, m : m + 1, :].to_broadcast(shape), op=ALU.mult,
-                )
-                nc.vector.tensor_tensor(
-                    out=with_sin[:, heads].rearrange("p h s j -> p h (s j)"),
-                    in0=u, in1=minus_plus_sin[:, m : m + 1, :].to_broadcast(shape), op=ALU.mult,
+                    out=products[:, :, heads, :], in0=u.unsqueeze(1).to_broadcast(shape),
+                    in1=trig[:, m].unsqueeze(2).to_broadcast(shape), op=ALU.mult,
                 )
 
             def first_share():
@@ -206,10 +205,10 @@ def tile_causalselfattention_pa_k_kernel(tc, x, w_qkv_tern, q_gain, out_0, out_1
                 nc.vector.tensor_reduce(out=sum_sq[:], in_=squares[:], axis=AXIS.X, op=ALU.add)
 
                 nc.vector.tensor_tensor(
-                    out=rotated[:, :, 0, :], in0=with_cos[:, :, 0, :], in1=with_sin[:, :, 1, :], op=ALU.add
+                    out=rotated[:, :, 0, :], in0=by_half[:, 0, :, 0, :], in1=by_half[:, 1, :, 1, :], op=ALU.add
                 )
                 nc.vector.tensor_tensor(
-                    out=rotated[:, :, 1, :], in0=with_cos[:, :, 1, :], in1=with_sin[:, :, 0, :], op=ALU.add
+                    out=rotated[:, :, 1, :], in0=by_half[:, 0, :, 1, :], in1=by_half[:, 1, :, 0, :], op=ALU.add
                 )
 
             def third_share():
@@ -238,13 +237,15 @@ def tile_causalselfattention_pa_k_kernel(tc, x, w_qkv_tern, q_gain, out_0, out_1
                     out_cols = q_out[:, :, rnd * GROUP_ROWS : (rnd + 1) * GROUP_ROWS]
                 else:
                     out_cols = k_out
-                nc.gpsimd.dma_start(out=out_cols, in_=result[:])
+                nc.sync.dma_start(out=out_cols, in_=result[:])
 
             return [first_share, second_share, third_share]
 
         for i in range(PREFETCH):
             load(i)
 
+        position = const.tile([P, TOKEN_TILES], I32)
+        nc.gpsimd.iota(position[:], pattern=[[P, TOKEN_TILES]], base=0, channel_multiplier=1)
         ident = const.tile([P, P], F32)
         masks.make_identity(nc, ident[:])
         gain_bf = const.tile([P, Q_HEADS], BF16)
@@ -252,15 +253,18 @@ def tile_causalselfattention_pa_k_kernel(tc, x, w_qkv_tern, q_gain, out_0, out_1
         eps = const.tile([P, 1], F32)
         nc.vector.memset(eps[:], RMS_EPS)
 
-        position_i = const.tile([P, TOKEN_TILES], I32)
-        nc.gpsimd.iota(position_i[:], pattern=[[P, TOKEN_TILES]], base=0, channel_multiplier=1)
-        position = const.tile([P, TOKEN_TILES], F32)
-        nc.vector.tensor_copy(out=position[:], in_=position_i[:])
         angle = const.tile([P, TOKEN_TILES, HALF], F32)
-        for j in range(HALF):
+        for j in range(ANGLES_ALONE):
             nc.vector.tensor_scalar_mul(
                 out=angle[:, :, j], in0=position[:], scalar1=ROPE_BASE ** (-2.0 * j / HEAD)
             )
+        made = ANGLES_ALONE
+        while made < HALF:
+            nc.vector.tensor_scalar_mul(
+                out=angle[:, :, made : 2 * made], in0=angle[:, :, :made],
+                scalar1=ROPE_BASE ** (-2.0 * made / HEAD),
+            )
+            made *= 2
         turns = const.tile([P, TOKEN_TILES, HALF], F32)
         nc.vector.tensor_scalar(
             out=turns[:], in0=angle[:], scalar1=1.0 / TWO_PI, scalar2=ROUND_MAGIC, op0=ALU.mult, op1=ALU.add
@@ -273,16 +277,17 @@ def tile_causalselfattention_pa_k_kernel(tc, x, w_qkv_tern, q_gain, out_0, out_1
         nc.vector.tensor_scalar(
             out=angle[:], in0=angle[:], scalar1=SIN_LIMIT, scalar2=-SIN_LIMIT, op0=ALU.min, op1=ALU.max
         )
-        minus_plus_sin = const.tile([P, TOKEN_TILES, HEAD], F32)
-        cos_cos = const.tile([P, TOKEN_TILES, HEAD], F32)
+        trig = const.tile([P, TOKEN_TILES, 2, HEAD], F32)
         sin_half = const.tile([P, TOKEN_TILES, HALF], F32)
         nc.scalar.activation(out=sin_half[:], in_=angle[:], func=ACT.Sin, scale=0.5)
-        nc.scalar.activation(out=minus_plus_sin[:, :, :HALF], in_=angle[:], func=ACT.Sin, scale=-1.0)
-        nc.scalar.activation(out=minus_plus_sin[:, :, HALF:], in_=angle[:], func=ACT.Sin)
+        nc.scalar.activation(out=trig[:, :, 1, :HALF], in_=angle[:], func=ACT.Sin, scale=-1.0)
+        nc.scalar.activation(out=trig[:, :, 1, HALF:], in_=angle[:], func=ACT.Sin)
+        table_first = const.tile([P, 1], F32)
+        nc.scalar.activation(out=table_first[:], in_=eps[:], func=ACT.Sqrt)
         nc.vector.tensor_tensor(out=sin_half[:], in0=sin_half[:], in1=sin_half[:], op=ALU.mult)
         for s in range(2):
             nc.vector.tensor_scalar(
-                out=cos_cos[:, :, s * HALF : (s + 1) * HALF], in0=sin_half[:],
+                out=trig[:, :, 0, s * HALF : (s + 1) * HALF], in0=sin_half[:],
                 scalar1=-2.0, scalar2=1.0, op0=ALU.mult, op1=ALU.add,
             )
 

import math
from contextlib import ExitStack

import concourse.masks as masks
import concourse.mybir as mybir

F32 = mybir.dt.float32
I32 = mybir.dt.int32
BF16 = mybir.dt.bfloat16
U32 = mybir.dt.uint32
U8 = mybir.dt.uint8
FP8X4 = mybir.dt.float8_e4m3fn_x4
ALU = mybir.AluOpType
ACT = mybir.ActivationFunctionType
AXIS = mybir.AxisListType

P = 128
PACK = 4
K_PASS = P * PACK
PLANES = 2

TOKENS = 256
DIM = 8192
HEAD = 64
HALF = HEAD // 2
Q_HEADS = 16
ROPE_BASE = 10000.0
ANGLES_ALONE = 8
RMS_EPS = 1.1920929e-07

ROW_TILES = 2
GROUP_ROWS = ROW_TILES * P
TOKEN_TILES = TOKENS // P
CHUNK_PASSES = 4
CHUNK_K = CHUNK_PASSES * K_PASS
K_PARTS = DIM // CHUNK_K
HEADS_PER_ROUND = GROUP_ROWS // HEAD
ROUND_HEADS = TOKEN_TILES * HEADS_PER_ROUND
Q_ROUNDS = Q_HEADS // HEADS_PER_ROUND
K_ROUND = Q_ROUNDS
V_ROUND = Q_ROUNDS + 1
ROUNDS = Q_ROUNDS + 2

PREFETCH = 8
RAW_BUFS = PREFETCH + 1
RUN_PARTS = 2
W_BUFS = 5
MX_ALIGN = 256
QUANT_PASSES = 2
TRANSPOSE_BANKS = 6
VECTOR_EVERY = 8

FLOPS = 2 * TOKENS * DIM * (Q_HEADS + 8) * HEAD

TWO_PI = 2.0 * math.pi
TWO_PI_HIGH = 6.283203125
TWO_PI_MID = -1.7814338207244873e-05
TWO_PI_LOW = TWO_PI - TWO_PI_HIGH - TWO_PI_MID
ROUND_MAGIC = 12582912.0
SIN_LIMIT = 3.1415925


def tile_causalselfattention_pa_k_kernel(tc, x, w_qkv_tern, q_gain, out_0, out_1, out_2):
    nc = tc.nc

    x_rows = x.rearrange("b (j p) k -> p (b j) k", p=P)
    w_rows = w_qkv_tern.rearrange("(r j p) k -> r p j k", j=ROW_TILES, p=P)
    q_out = out_0.rearrange("b (m p) h d -> p (b m) (h d)", p=P)
    k_out = out_1.rearrange("b (m p) h d -> p (b m) (h d)", p=P)
    v_out = out_2.rearrange("b (m p) h d -> p (b m) (h d)", p=P)

    chunks = []
    for part in range(K_PARTS):
        chunks.append((None, part))
        chunks.append((0, part))
    for rnd in range(1, ROUNDS):
        for part in range(K_PARTS):
            chunks.append((rnd, part))

    with ExitStack() as ctx:
        const = ctx.enter_context(tc.tile_pool(name="const", bufs=1))
        raw_pool = ctx.enter_context(tc.tile_pool(name="raw", bufs=RAW_BUFS))
        grouped_pool = ctx.enter_context(tc.tile_pool(name="grouped", bufs=6))
        w_pool = ctx.enter_context(tc.tile_pool(name="w_mx", bufs=W_BUFS))
        post = ctx.enter_context(tc.tile_pool(name="post", bufs=2))
        result_pool = ctx.enter_context(tc.tile_pool(name="results", bufs=ROUNDS))
        bank_pool = ctx.enter_context(tc.psum_pool(name="banks", bufs=TRANSPOSE_BANKS))
        sum_pool = ctx.enter_context(tc.psum_pool(name="sums", bufs=1))
        ctx.enter_context(tc.manual_schedule())

        raws = {}
        mx = {}
        x_mx = {}
        sums = {}

        def load(i):
            rnd, part = chunks[i]
            rows = x_rows if rnd is None else w_rows[rnd]
            raw = raw_pool.tile([P, ROW_TILES * CHUNK_K], BF16)
            raw_rows = raw[:].rearrange("p (j k) -> p j k", j=ROW_TILES)
            nc.sync.dma_start(out=raw_rows, in_=rows[:, :, part * CHUNK_K : (part + 1) * CHUNK_K])
            raws[i] = raw

        def quantise(grouped, words, scales, n, size):
            cols = slice(n * size * GROUP_ROWS, (n + 1) * size * GROUP_ROWS)
            nc.vector.quantize_mx(
                out=words[:, cols].bitcast(FP8X4), scales=scales[:, cols], in_=grouped[:]
            )

        def stage(i):
            rnd, part = chunks[i]
            pool = const if rnd is None else w_pool
            words = pool.tile(
                [P, CHUNK_PASSES * GROUP_ROWS], U32, align_bytes=MX_ALIGN,
                name="x_words%d" % part if rnd is None else "w_words",
            )
            scales = pool.tile(
                [P, CHUNK_PASSES * GROUP_ROWS], U8, align_bytes=MX_ALIGN,
                name="x_scales%d" % part if rnd is None else "w_scales",
            )
            if rnd is None:
                x_mx[part] = (words, scales)
            else:
                mx[i] = (words, scales)
            raw_words = raws[i][:].bitcast(F32).rearrange("p (j w) -> p j w", j=ROW_TILES)
            waiting = None
            is_last = i == len(chunks) - 1
            size = 1 if is_last else QUANT_PASSES
            for n in range(CHUNK_PASSES // size):
                grouped = grouped_pool.tile([P, size * GROUP_ROWS * PACK], BF16, align_bytes=MX_ALIGN)
                grouped_words = grouped[:].bitcast(F32).rearrange(
                    "p (c j n u) -> p c j n u", c=size, j=ROW_TILES, u=PLANES
                )
                for c in range(size):
                    g = n * size + c
                    bank = bank_pool.tile([P, ROW_TILES, PLANES, P], F32)
                    for j in range(ROW_TILES):
                        for u in range(PLANES):
                            w0 = (g * PLANES + u) * P
                            nc.tensor.transpose(
                                out=bank[:, j, u, :], in_=raw_words[:, j, w0 : w0 + P], identity=ident[:]
                            )
                    to_vector = g == 1 if is_last else (part * CHUNK_PASSES + g) % VECTOR_EVERY == VECTOR_EVERY - 1
                    empty = nc.vector.tensor_copy if to_vector else nc.scalar.copy
                    empty(out=grouped_words[:, c], in_=bank[:].rearrange("p j u n -> p j n u"))
                if waiting is not None:
                    quantise(waiting, words, scales, n - 1, size)
                waiting = grouped
            quantise(waiting, words, scales, n, size)

        def multiply(i):
            rnd, part = chunks[i]
            if part == 0:
                sums[rnd] = [
                    sum_pool.tile([P, GROUP_ROWS], F32, name="sum%d" % m) for m in range(TOKEN_TILES)
                ]
            w_words, w_scales = mx[i]
            x_words, x_scales = x_mx[part]
            for g in range(CHUNK_PASSES):
                w_cols = slice(g * GROUP_ROWS, (g + 1) * GROUP_ROWS)
                for m in range(TOKEN_TILES):
                    x_cols = slice(g * TOKENS + m * P, g * TOKENS + (m + 1) * P)
                    nc.tensor.matmul_mx(
                        out=sums[rnd][m][:],
                        lhsT=x_words[:, x_cols].bitcast(FP8X4),
                        lhsT_scale=x_scales[:, x_cols],
                        rhs=w_words[:, w_cols].bitcast(FP8X4),
                        rhs_scale=w_scales[:, w_cols],
                        start=(part == 0 and g == 0),
                        stop=(part == K_PARTS - 1 and g == CHUNK_PASSES - 1),
                    )

        def v_leaves(rnd):
            acc = sums[rnd]
            halves = [post.tile([P, GROUP_ROWS], F32, name="v_result%d" % m) for m in range(TOKEN_TILES)]
            nc.scalar.copy(out=halves[0][:], in_=acc[0][:])
            nc.vector.tensor_copy(out=halves[1][:], in_=acc[1][:])
            nc.scalar.dma_start(out=v_out[:, 0, :], in_=halves[0][:])
            nc.sync.dma_start(out=v_out[:, 1, :], in_=halves[1][:])

        def epilogue(rnd):
            acc = sums[rnd]
            squares = post.tile([P, ROUND_HEADS, HEAD], F32)
            products = post.tile([P, 2, ROUND_HEADS, HEAD], F32)
            by_half = products[:].rearrange("p t h (s j) -> p t h s j", s=2)
            rotated = post.tile([P, ROUND_HEADS, 2, HALF], F32)
            sum_sq = post.tile([P, ROUND_HEADS], F32)
            factor = post.tile([P, ROUND_HEADS], F32)

            def leave_psum(m):
                heads = slice(m * HEADS_PER_ROUND, (m + 1) * HEADS_PER_ROUND)
                u = acc[m][:].rearrange("p (h d) -> p h d", d=HEAD)
                shape = [P, 2, HEADS_PER_ROUND, HEAD]
                nc.scalar.activation(out=squares[:, heads, :], in_=u, func=ACT.Square)
                nc.vector.tensor_tensor(
                    out=products[:, :, heads, :], in0=u.unsqueeze(1).to_broadcast(shape),
                    in1=trig[:, m].unsqueeze(2).to_broadcast(shape), op=ALU.mult,
                )

            def first_share():
                for m in range(TOKEN_TILES):
                    leave_psum(m)

            def second_share():
                nc.vector.tensor_reduce(out=sum_sq[:], in_=squares[:], axis=AXIS.X, op=ALU.add)

                nc.vector.tensor_tensor(
                    out=rotated[:, :, 0, :], in0=by_half[:, 0, :, 0, :], in1=by_half[:, 1, :, 1, :], op=ALU.add
                )
                nc.vector.tensor_tensor(
                    out=rotated[:, :, 1, :], in0=by_half[:, 0, :, 1, :], in1=by_half[:, 1, :, 0, :], op=ALU.add
                )

            def third_share():
                result = result_pool.tile([P, TOKEN_TILES, GROUP_ROWS], F32)
                nc.scalar.activation(
                    out=factor[:], in_=sum_sq[:], func=ACT.Sqrt, scale=1.0 / HEAD, bias=eps[:, 0:1]
                )
                nc.vector.reciprocal(out=factor[:], in_=factor[:])
                if rnd < Q_ROUNDS:
                    by_tile = factor[:].rearrange("p (m h) -> p m h", m=TOKEN_TILES)
                    h0 = rnd * HEADS_PER_ROUND
                    nc.vector.tensor_tensor(
                        out=by_tile, in0=by_tile,
                        in1=gain[:, h0 : h0 + HEADS_PER_ROUND].unsqueeze(1).to_broadcast(
                            [P, TOKEN_TILES, HEADS_PER_ROUND]
                        ),
                        op=ALU.mult,
                    )
                nc.vector.tensor_tensor(
                    out=result[:].rearrange("p m (h d) -> p (m h) d", d=HEAD),
                    in0=rotated[:].rearrange("p g s j -> p g (s j)"),
                    in1=factor[:].unsqueeze(2).to_broadcast([P, ROUND_HEADS, HEAD]),
                    op=ALU.mult,
                )
                if rnd < Q_ROUNDS:
                    out_cols = q_out[:, :, rnd * GROUP_ROWS : (rnd + 1) * GROUP_ROWS]
                else:
                    out_cols = k_out
                nc.sync.dma_start(out=out_cols, in_=result[:])

            return [first_share, second_share, third_share]

        for i in range(PREFETCH):
            load(i)

        position = const.tile([P, TOKEN_TILES], I32)
        nc.gpsimd.iota(position[:], pattern=[[P, TOKEN_TILES]], base=0, channel_multiplier=1)
        ident = const.tile([P, P], F32)
        masks.make_identity(nc, ident[:])
        gain_bf = const.tile([P, Q_HEADS], BF16)
        nc.scalar.dma_start(out=gain_bf[:], in_=q_gain.partition_broadcast(P))
        eps = const.tile([P, 1], F32)
        nc.vector.memset(eps[:], RMS_EPS)

        angle = const.tile([P, TOKEN_TILES, HALF], F32)
        for j in range(ANGLES_ALONE):
            nc.vector.tensor_scalar_mul(
                out=angle[:, :, j], in0=position[:], scalar1=ROPE_BASE ** (-2.0 * j / HEAD)
            )
        made = ANGLES_ALONE
        while made < HALF:
            nc.vector.tensor_scalar_mul(
                out=angle[:, :, made : 2 * made], in0=angle[:, :, :made],
                scalar1=ROPE_BASE ** (-2.0 * made / HEAD),
            )
            made *= 2
        turns = const.tile([P, TOKEN_TILES, HALF], F32)
        nc.vector.tensor_scalar(
            out=turns[:], in0=angle[:], scalar1=1.0 / TWO_PI, scalar2=ROUND_MAGIC, op0=ALU.mult, op1=ALU.add
        )
        nc.vector.tensor_scalar_sub(out=turns[:], in0=turns[:], scalar1=ROUND_MAGIC)
        for piece in (TWO_PI_HIGH, TWO_PI_MID, TWO_PI_LOW):
            nc.vector.scalar_tensor_tensor(
                out=angle[:], in0=turns[:], scalar=-piece, in1=angle[:], op0=ALU.mult, op1=ALU.add
            )
        nc.vector.tensor_scalar(
            out=angle[:], in0=angle[:], scalar1=SIN_LIMIT, scalar2=-SIN_LIMIT, op0=ALU.min, op1=ALU.max
        )
        trig = const.tile([P, TOKEN_TILES, 2, HEAD], F32)
        sin_half = const.tile([P, TOKEN_TILES, HALF], F32)
        nc.scalar.activation(out=sin_half[:], in_=angle[:], func=ACT.Sin, scale=0.5)
        nc.scalar.activation(out=trig[:, :, 1, :HALF], in_=angle[:], func=ACT.Sin, scale=-1.0)
        nc.scalar.activation(out=trig[:, :, 1, HALF:], in_=angle[:], func=ACT.Sin)
        table_first = const.tile([P, 1], F32)
        nc.scalar.activation(out=table_first[:], in_=eps[:], func=ACT.Sqrt)
        nc.vector.tensor_tensor(out=sin_half[:], in0=sin_half[:], in1=sin_half[:], op=ALU.mult)
        for s in range(2):
            nc.vector.tensor_scalar(
                out=trig[:, :, 0, s * HALF : (s + 1) * HALF], in0=sin_half[:],
                scalar1=-2.0, scalar2=1.0, op0=ALU.mult, op1=ALU.add,
            )

        gain = const.tile([P, Q_HEADS], F32)
        nc.vector.tensor_copy(out=gain[:], in_=gain_bf[:])

        shares = []
        for i in range(len(chunks) + 1):
            if i + PREFETCH < len(chunks):
                load(i + PREFETCH)
            if i < len(chunks):
                stage(i)
            if shares:
                shares.pop(0)()
            if i == 0 or chunks[i - 1][0] is None:
                continue
            rnd, part = chunks[i - 1]
            if rnd == 0:
                multiply(i - 1)
            elif part % RUN_PARTS == RUN_PARTS - 1:
                for j in range(i - RUN_PARTS, i):
                    multiply(j)
            if part == K_PARTS - 1:
                if rnd == V_ROUND:
                    v_leaves(rnd)
                else:
                    shares = epilogue(rnd)
                    shares.pop(0)()
